import numpy as np
import ml_dtypes


def mxq(x, axis, fmt="e4m3"):
    dtype, down = {"e4m3": (ml_dtypes.float8_e4m3fn, 7), "e5m2": (ml_dtypes.float8_e5m2, 14)}[fmt]
    v = np.moveaxis(np.asarray(x, np.float32).astype(ml_dtypes.bfloat16).astype(np.float64), axis, -1)
    blocks = v.reshape(v.shape[:-1] + (-1, 32))
    amax = np.abs(blocks).max(-1, keepdims=True)
    byte = np.maximum(np.where(amax > 0, np.frexp(amax)[1] - 1 + 127, 0) - down, 1)
    scale = np.exp2(byte - 127.0)
    codes = (blocks / scale).astype(np.float32).astype(dtype).astype(np.float64)
    return np.moveaxis((codes * scale).reshape(v.shape), -1, axis)


WIDE = False


def mx_kscale(k):
    if not WIDE:
        return np.ones(k)
    levels = np.array([10, -10, 5, -5, 0])
    a = np.random.permutation(np.resize(levels, k // 512 * 4)).reshape(k // 512, 4)
    idx = np.arange(k)
    return np.exp2(a[idx // 512, idx % 128 // 32])


BF16 = ml_dtypes.bfloat16


def bf(x):
    return np.asarray(x, np.float32).astype(BF16)


def f64(x):
    return np.asarray(x).astype(np.float64)


M, K, P, Q = 256, 2048, 128, 16
N = P * Q
SCALING = 2.0


def _kron(A, B):
    m, n = A.shape
    p, q = B.shape
    return (A[:, None, :, None] * B[None, :, None, :]).reshape(m * p, n * q)


def setup_inputs():
    s = mx_kscale(K)
    return {"x": bf(np.random.standard_normal((M, K)) * s),
            "original_weight": bf(np.random.standard_normal((N, K)) / np.sqrt(K) / s),
            "lokr_A": bf(np.random.standard_normal((P, K)) / np.sqrt(K) / s),
            "lokr_B": bf(np.random.standard_normal((Q, 1)) * 0.25),
            "scalar": bf(1.5 + 0.1 * np.random.standard_normal(1))}


def reference(x, original_weight, lokr_A, lokr_B, scalar):
    delta_W = _kron(f64(lokr_A), f64(lokr_B)) * SCALING
    W_eff = f64(original_weight) + f64(scalar)[0] * delta_W
    return mxq(f64(x), 1, "e4m3") @ mxq(W_eff, 1, "e4m3").T

@@ -1,0 +1,230 @@
+from contextlib import ExitStack
+
+import concourse.mybir as mybir
+from concourse.masks import make_identity
+
+FP8X4 = mybir.dt.float8_e4m3fn_x4
+BF16 = mybir.dt.bfloat16
+F32 = mybir.dt.float32
+U32 = mybir.dt.uint32
+U8 = mybir.dt.uint8
+ALU = mybir.AluOpType
+
+FLOPS = 2 * 256 * 2048 * 2048
+
+P = 128
+NG = 4
+LOOKAHEAD = 4
+W_PIECES = [(0, 0, 1), (0, 1, 1), (0, 2, 2), (0, 4, 4), (0, 8, 4), (0, 12, 4),
+            (1, 0, 4), (1, 4, 4), (1, 8, 4), (1, 12, 4)]
+X_AFTER_PIECE = 3
+CHUNKS = [(0, 0, 8), (0, 8, 8), (1, 0, 8), (1, 8, 4), (1, 12, 2), (1, 14, 2)]
+
+
+def tile_lokrlayer_kernel(tc, x, original_weight, lokr_A, lokr_B, scalar, out):
+    nc = tc.nc
+    with ExitStack() as ctx:
+        const = ctx.enter_context(tc.tile_pool(name="const", bufs=1))
+        wpool = ctx.enter_context(tc.tile_pool(name="wpool", bufs=1))
+        gpool = ctx.enter_context(tc.tile_pool(name="gpool", bufs=2))
+        cpool = ctx.enter_context(tc.tile_pool(name="cpool", bufs=1))
+        opool = ctx.enter_context(tc.tile_pool(name="opool", bufs=1))
+        tpp = ctx.enter_context(tc.psum_pool(name="tpp", bufs=5))
+        accp = ctx.enter_context(tc.psum_pool(name="accp", bufs=3))
+        ctx.enter_context(tc.manual_schedule())
+
+        ident = const.tile([P, P], F32, name="ident")
+        make_identity(nc, ident[:])
+
+        b_bc = const.tile([P, 16], BF16, name="b_bc")
+        nc.scalar.dma_start(out=b_bc[:], in_=lokr_B.rearrange("q o -> (q o)").partition_broadcast(P))
+        s_bc = const.tile([P, 1], BF16, name="s_bc")
+        nc.scalar.dma_start(out=s_bc[:], in_=scalar.partition_broadcast(P))
+
+        a_sb = const.tile([P, 2048], BF16, name="a_sb")
+        nc.sync.dma_start(out=a_sb[:], in_=lokr_A)
+
+        wv = original_weight.rearrange(
+            "(h r q) (g u j) -> h u r q g j", h=2, r=64, q=16, g=NG, u=2, j=256
+        )
+        x_sb = []
+        unit_src = {}
+        for n, (h, q0, nq) in enumerate(W_PIECES):
+            wt = wpool.tile([P, nq * 1024], BF16, name="wt%d" % n)
+            for u in range(2):
+                nc.sync.dma_start(
+                    out=wt[u:P:2, :].rearrange("r (q g j) -> r q g j", q=nq, g=NG, j=256),
+                    in_=wv[h, u, :, q0:q0 + nq],
+                )
+            for ql in range(nq):
+                unit_src[h * 16 + q0 + ql] = (wt, ql)
+            if n == X_AFTER_PIECE:
+                for mt in range(2):
+                    xt = const.tile([P, 2048], BF16, name="x_sb%d" % mt)
+                    nc.sync.dma_start(out=xt[:], in_=x[mt * P:(mt + 1) * P, :])
+                    x_sb.append(xt)
+
+        s32 = const.tile([P, 1], F32, name="s32")
+        nc.vector.tensor_copy(out=s32[:], in_=s_bc[:])
+        cb = const.tile([P, 16], F32, name="cb")
+        nc.vector.tensor_scalar(
+            out=cb[:], in0=b_bc[:], scalar1=s32[:, 0:1], scalar2=2.0, op0=ALU.mult, op1=ALU.mult
+        )
+
+        at = const.tile([P, 2048], BF16, name="at")
+        at_w = at[:].bitcast(F32)
+        a_w = a_sb[:].bitcast(F32)
+        for b in range(2):
+            pa = accp.tile([P, 512], F32, name="pa%d" % b, tag="acc")
+            for g2 in range(2):
+                for u in range(2):
+                    w0 = 256 * (2 * b + g2) + 128 * u
+                    c0 = (g2 * 2 + u) * P
+                    nc.tensor.transpose(out=pa[:, c0:c0 + P], in_=a_w[:, w0:w0 + P], identity=ident[:])
+            src = pa[:].rearrange("p (g u h r) -> p h g r u", g=2, u=2, h=2, r=64)
+            for h in range(2):
+                d0 = (h * NG + 2 * b) * P
+                dst = at_w[:, d0:d0 + 2 * P].rearrange("p (g r u) -> p g r u", g=2, r=64, u=2)
+                if b == 0:
+                    nc.scalar.copy(out=dst, in_=src[:, h])
+                else:
+                    nc.vector.tensor_copy(out=dst, in_=src[:, h])
+        at_v = at[:].rearrange("p (h g j) -> p h g j", h=2, g=NG, j=256)
+
+        xg = const.tile([P, 4096], BF16, name="xg", align_bytes=64)
+        xg_w = xg[:].bitcast(F32)
+        x_codes = const.tile([P, 1024], U32, name="x_codes", align_bytes=64)
+        x_scales = const.tile([P, 1024], U8, name="x_scales", align_bytes=64)
+
+        def transpose_x():
+            for g in range(NG):
+                px = accp.tile([P, 512], F32, name="px%d" % g, tag="acc")
+                for u in range(2):
+                    for mt in range(2):
+                        w0 = 256 * g + 128 * u
+                        c0 = (u * 2 + mt) * P
+                        nc.tensor.transpose(
+                            out=px[:, c0:c0 + P],
+                            in_=x_sb[mt][:].bitcast(F32)[:, w0:w0 + P],
+                            identity=ident[:],
+                        )
+                nc.scalar.copy(
+                    out=xg_w[:, g * 512:(g + 1) * 512].rearrange("p (c u) -> p c u", u=2),
+                    in_=px[:].rearrange("p (u c) -> p c u", u=2),
+                )
+
+        def quantise_x():
+            nc.vector.quantize_mx(out=x_codes[:].bitcast(FP8X4), scales=x_scales[:], in_=xg[:])
+
+        banks = {}
+
+        def transpose_unit(i):
+            wt, ql = unit_src[i]
+            ww = wt[:].bitcast(F32)
+            bank = tpp.tile([P, 512], F32, name="tp%d" % i, tag="tp")
+            for g in range(NG):
+                w0 = (ql * NG + g) * P
+                nc.tensor.transpose(out=bank[:, g * P:(g + 1) * P], in_=ww[:, w0:w0 + P], identity=ident[:])
+            banks[i] = bank
+
+        chunk_of = {}
+        chunk_tiles = []
+        for c, (h, q0, nq) in enumerate(CHUNKS):
+            for ql in range(nq):
+                chunk_of[h * 16 + q0 + ql] = (c, ql)
+            chunk_tiles.append(None)
+
+        def open_chunk(c):
+            nq = CHUNKS[c][2]
+            grouped = gpool.tile([P, NG, nq, 256], BF16, name="grouped%d" % c, tag="grouped", align_bytes=64)
+            codes = cpool.tile([P, NG, nq * 64], U32, name="codes%d" % c, align_bytes=64)
+            scales = cpool.tile([P, NG, nq * 64], U8, name="scales%d" % c, align_bytes=64)
+            chunk_tiles[c] = (grouped, codes, scales)
+
+        def combine_unit(i):
+            c, ql = chunk_of[i]
+            if ql == 0:
+                open_chunk(c)
+            grouped = chunk_tiles[c][0]
+            h, q = i // 16, i % 16
+            nc.vector.scalar_tensor_tensor(
+                out=grouped[:, :, ql, :],
+                in0=at_v[:, h],
+                scalar=cb[:, q:q + 1],
+                in1=banks[i][:].bitcast(BF16).rearrange("p (g j) -> p g j", g=NG),
+                op0=ALU.mult,
+                op1=ALU.add,
+            )
+
+        def quantise_chunk(c, part, parts):
+            grouped, codes, scales = chunk_tiles[c]
+            n = NG // parts
+            g0 = part * n
+            nc.vector.quantize_mx(
+                out=codes[:, g0:g0 + n, :].rearrange("p g n -> p (g n)").bitcast(FP8X4),
+                scales=scales[:, g0:g0 + n, :].rearrange("p g n -> p (g n)"),
+                in_=grouped[:, g0:g0 + n, :, :].rearrange("p g q j -> p (g q j)"),
+            )
+
+        out_sb = {}
+        for h in range(2):
+            for mt in range(2):
+                out_sb[(h, mt)] = opool.tile([P, 64, 16], F32, name="out_sb%d%d" % (h, mt))
+
+        def multiply_chunk(c):
+            h, q0, nq = CHUNKS[c]
+            codes, scales = chunk_tiles[c][1], chunk_tiles[c][2]
+            accs = []
+            for mt in range(2):
+                acc = accp.tile([P, nq * 64], F32, name="acc%d_%d" % (c, mt), tag="acc")
+                accs.append(acc)
+            for g in range(NG):
+                for mt in range(2):
+                    m0 = g * 256 + mt * P
+                    nc.tensor.matmul_mx(
+                        out=accs[mt][:],
+                        lhsT=x_codes[:, m0:m0 + P].bitcast(FP8X4),
+                        lhsT_scale=x_scales[:, m0:m0 + P],
+                        rhs=codes[:, g, :].bitcast(FP8X4),
+                        rhs_scale=scales[:, g, :],
+                        start=(g == 0),
+                        stop=(g == NG - 1),
+                    )
+            for mt in range(2):
+                dst = out_sb[(h, mt)][:, :, q0:q0 + nq]
+                src = accs[mt][:].rearrange("m (q r) -> m r q", q=nq)
+                nc.scalar.copy(out=dst, in_=src)
+            if q0 + nq == 16:
+                for mt in range(2):
+                    nc.sync.dma_start(
+                        out=out[mt * P:(mt + 1) * P, h * 1024:(h + 1) * 1024],
+                        in_=out_sb[(h, mt)][:].rearrange("m r q -> m (r q)"),
+                    )
+
+        n_units = 32
+        after = {}
+        for i in range(n_units):
+            after[i] = []
+        after[5].append(transpose_x)
+        after[10].append(quantise_x)
+        for c, (h, q0, nq) in enumerate(CHUNKS):
+            end = h * 16 + q0 + nq - 1
+            parts = 2 if nq == 8 else 1
+            for part in range(parts):
+                at_unit = min(end + 2 * (part + 1), n_units - 1)
+                after[at_unit].append((c, part, parts))
+
+        for i in range(LOOKAHEAD):
+            transpose_unit(i)
+        for i in range(n_units):
+            if i + LOOKAHEAD < n_units:
+                transpose_unit(i + LOOKAHEAD)
+            combine_unit(i)
+            for job in after[i]:
+                if isinstance(job, tuple):
+                    c, part, parts = job
+                    quantise_chunk(c, part, parts)
+                    if part == parts - 1:
+                        multiply_chunk(c)
+                else:
+                    job()

@@ -9,16 +9,26 @@ F32 = mybir.dt.float32
 U32 = mybir.dt.uint32
 U8 = mybir.dt.uint8
 ALU = mybir.AluOpType
+ACT = mybir.ActivationFunctionType
 
 FLOPS = 2 * 256 * 2048 * 2048
 
 P = 128
 NG = 4
-LOOKAHEAD = 4
-W_PIECES = [(0, 0, 1), (0, 1, 1), (0, 2, 2), (0, 4, 4), (0, 8, 4), (0, 12, 4),
+N_UNITS = 32
+TP_BANKS = 6
+W_PIECES = [(0, 0, 1), (0, 1, 1), (0, 2, 2), (0, 4, 2), (0, 6, 2), (0, 8, 4), (0, 12, 4),
             (1, 0, 4), (1, 4, 4), (1, 8, 4), (1, 12, 4)]
-X_AFTER_PIECE = 3
-CHUNKS = [(0, 0, 8), (0, 8, 8), (1, 0, 8), (1, 8, 4), (1, 12, 2), (1, 14, 2)]
+X_AFTER_PIECE = 6
+PHASES = [
+    [(0, 0, 8, "ga"), (0, 8, 8, "gb")],
+    [(1, 0, 8, "gb"), (1, 8, 4, "ga")],
+    [(1, 12, 4, "ga")],
+]
+ROUND = 3
+STAGE_AHEAD = 3
+X_TRANSPOSE_AFTER = 15
+LATE_COPY_AFTER = 19
 
 
 def tile_lokrlayer_kernel(tc, x, original_weight, lokr_A, lokr_B, scalar, out):
@@ -26,11 +36,12 @@ def tile_lokrlayer_kernel(tc, x, original_weight, lokr_A, lokr_B, scalar, out):
     with ExitStack() as ctx:
         const = ctx.enter_context(tc.tile_pool(name="const", bufs=1))
         wpool = ctx.enter_context(tc.tile_pool(name="wpool", bufs=1))
-        gpool = ctx.enter_context(tc.tile_pool(name="gpool", bufs=2))
+        gpool = ctx.enter_context(tc.tile_pool(name="gpool", bufs=1))
+        spool = ctx.enter_context(tc.tile_pool(name="spool", bufs=3))
         cpool = ctx.enter_context(tc.tile_pool(name="cpool", bufs=1))
         opool = ctx.enter_context(tc.tile_pool(name="opool", bufs=1))
-        tpp = ctx.enter_context(tc.psum_pool(name="tpp", bufs=5))
-        accp = ctx.enter_context(tc.psum_pool(name="accp", bufs=3))
+        tpp = ctx.enter_context(tc.psum_pool(name="tpp", bufs=TP_BANKS))
+        accp = ctx.enter_context(tc.psum_pool(name="accp", bufs=2))
         ctx.enter_context(tc.manual_schedule())
 
         ident = const.tile([P, P], F32, name="ident")
@@ -74,6 +85,7 @@ def tile_lokrlayer_kernel(tc, x, original_weight, lokr_A, lokr_B, scalar, out):
         at = const.tile([P, 2048], BF16, name="at")
         at_w = at[:].bitcast(F32)
         a_w = a_sb[:].bitcast(F32)
+        pas = []
         for b in range(2):
             pa = accp.tile([P, 512], F32, name="pa%d" % b, tag="acc")
             for g2 in range(2):
@@ -81,14 +93,19 @@ def tile_lokrlayer_kernel(tc, x, original_weight, lokr_A, lokr_B, scalar, out):
                     w0 = 256 * (2 * b + g2) + 128 * u
                     c0 = (g2 * 2 + u) * P
                     nc.tensor.transpose(out=pa[:, c0:c0 + P], in_=a_w[:, w0:w0 + P], identity=ident[:])
-            src = pa[:].rearrange("p (g u h r) -> p h g r u", g=2, u=2, h=2, r=64)
-            for h in range(2):
-                d0 = (h * NG + 2 * b) * P
-                dst = at_w[:, d0:d0 + 2 * P].rearrange("p (g r u) -> p g r u", g=2, r=64, u=2)
-                if b == 0:
-                    nc.scalar.copy(out=dst, in_=src[:, h])
-                else:
-                    nc.vector.tensor_copy(out=dst, in_=src[:, h])
+            pas.append(pa)
+
+        def copy_at(b, h):
+            src = pas[b][:].rearrange("p (g u h r) -> p h g r u", g=2, u=2, h=2, r=64)
+            d0 = (h * NG + 2 * b) * P
+            dst = at_w[:, d0:d0 + 2 * P].rearrange("p (g r u) -> p g r u", g=2, r=64, u=2)
+            if b == 0:
+                nc.scalar.copy(out=dst, in_=src[:, h])
+            else:
+                nc.vector.tensor_copy(out=dst, in_=src[:, h])
+
+        copy_at(0, 0)
+        copy_at(1, 0)
         at_v = at[:].rearrange("p (h g j) -> p h g j", h=2, g=NG, j=256)
 
         xg = const.tile([P, 4096], BF16, name="xg", align_bytes=64)
@@ -116,55 +133,97 @@ def tile_lokrlayer_kernel(tc, x, original_weight, lokr_A, lokr_B, scalar, out):
         def quantise_x():
             nc.vector.quantize_mx(out=x_codes[:].bitcast(FP8X4), scales=x_scales[:], in_=xg[:])
 
-        banks = {}
-
-        def transpose_unit(i):
-            wt, ql = unit_src[i]
-            ww = wt[:].bitcast(F32)
-            bank = tpp.tile([P, 512], F32, name="tp%d" % i, tag="tp")
-            for g in range(NG):
-                w0 = (ql * NG + g) * P
-                nc.tensor.transpose(out=bank[:, g * P:(g + 1) * P], in_=ww[:, w0:w0 + P], identity=ident[:])
-            banks[i] = bank
-
         chunk_of = {}
-        chunk_tiles = []
-        for c, (h, q0, nq) in enumerate(CHUNKS):
-            for ql in range(nq):
-                chunk_of[h * 16 + q0 + ql] = (c, ql)
-            chunk_tiles.append(None)
+        chunks = []
+        on_pool = {}
+        phase_end = {}
+        for phase in PHASES:
+            units = []
+            for (h, q0, nq, tag) in phase:
+                for ql in range(nq):
+                    chunk_of[h * 16 + q0 + ql] = (len(chunks), ql)
+                    units.append(h * 16 + q0 + ql)
+                chunks.append((h, q0, nq, tag))
+            for idx, i in enumerate(units):
+                on_pool[i] = idx % ROUND == 0 and idx + ROUND <= len(units)
+            phase_end[units[-1]] = phase
+        chunk_tiles = [None for c in chunks]
 
-        def open_chunk(c):
-            nq = CHUNKS[c][2]
-            grouped = gpool.tile([P, NG, nq, 256], BF16, name="grouped%d" % c, tag="grouped", align_bytes=64)
-            codes = cpool.tile([P, NG, nq * 64], U32, name="codes%d" % c, align_bytes=64)
-            scales = cpool.tile([P, NG, nq * 64], U8, name="scales%d" % c, align_bytes=64)
-            chunk_tiles[c] = (grouped, codes, scales)
+        banks = {}
+        used = {}
+        state = {"next": 0}
 
-        def combine_unit(i):
+        def transpose_ready_units():
+            while state["next"] < N_UNITS and (
+                state["next"] < TP_BANKS or used.get(state["next"] - TP_BANKS, False)
+            ):
+                i = state["next"]
+                wt, ql = unit_src[i]
+                ww = wt[:].bitcast(F32)
+                bank = tpp.tile([P, 512], F32, name="tp%d" % i, tag="tp")
+                for g in range(NG):
+                    w0 = (ql * NG + g) * P
+                    nc.tensor.transpose(
+                        out=bank[:, g * P:(g + 1) * P], in_=ww[:, w0:w0 + P], identity=ident[:]
+                    )
+                banks[i] = bank
+                state["next"] = i + 1
+
+        def grouped_slice(i):
             c, ql = chunk_of[i]
-            if ql == 0:
-                open_chunk(c)
-            grouped = chunk_tiles[c][0]
+            if chunk_tiles[c] is None:
+                nq, tag = chunks[c][2], chunks[c][3]
+                grouped = gpool.tile([P, NG, nq, 256], BF16, name="grouped%d" % c, tag=tag, align_bytes=64)
+                codes = cpool.tile([P, NG, nq * 64], U32, name="codes%d" % c, align_bytes=64)
+                scales = cpool.tile([P, NG, nq * 64], U8, name="scales%d" % c, align_bytes=64)
+                chunk_tiles[c] = (grouped, codes, scales)
+            return chunk_tiles[c][0][:, :, ql, :]
+
+        def combine_on_vector(i):
             h, q = i // 16, i % 16
             nc.vector.scalar_tensor_tensor(
-                out=grouped[:, :, ql, :],
+                out=grouped_slice(i),
                 in0=at_v[:, h],
                 scalar=cb[:, q:q + 1],
                 in1=banks[i][:].bitcast(BF16).rearrange("p (g j) -> p g j", g=NG),
                 op0=ALU.mult,
                 op1=ALU.add,
             )
+            used[i] = True
 
-        def quantise_chunk(c, part, parts):
-            grouped, codes, scales = chunk_tiles[c]
-            n = NG // parts
-            g0 = part * n
-            nc.vector.quantize_mx(
-                out=codes[:, g0:g0 + n, :].rearrange("p g n -> p (g n)").bitcast(FP8X4),
-                scales=scales[:, g0:g0 + n, :].rearrange("p g n -> p (g n)"),
-                in_=grouped[:, g0:g0 + n, :, :].rearrange("p g q j -> p (g q j)"),
+        staged = {}
+
+        def stage_for_pool(i):
+            h, q = i // 16, i % 16
+            delta = spool.tile([P, 1024], F32, name="delta%d" % i, tag="delta")
+            nc.scalar.activation(
+                out=delta[:], in_=at[:, h * 1024:(h + 1) * 1024], func=ACT.Copy, scale=cb[:, q:q + 1]
             )
+            wts = spool.tile([P, 512], F32, name="wts%d" % i, tag="wts")
+            nc.scalar.copy(out=wts[:], in_=banks[i][:])
+            staged[i] = (wts, delta)
+            used[i] = True
+
+        def combine_on_pool(i):
+            wts, delta = staged[i]
+            nc.gpsimd.tensor_tensor(
+                out=grouped_slice(i),
+                in0=wts[:].bitcast(BF16).rearrange("p (g j) -> p g j", g=NG),
+                in1=delta[:].rearrange("p (g j) -> p g j", g=NG),
+                op=ALU.add,
+            )
+
+        def quantise_chunk(c):
+            grouped, codes, scales = chunk_tiles[c]
+            parts = 2 if chunks[c][2] == 8 else 1
+            n = NG // parts
+            for part in range(parts):
+                g0 = part * n
+                nc.vector.quantize_mx(
+                    out=codes[:, g0:g0 + n, :].rearrange("p g n -> p (g n)").bitcast(FP8X4),
+                    scales=scales[:, g0:g0 + n, :].rearrange("p g n -> p (g n)"),
+                    in_=grouped[:, g0:g0 + n, :, :].rearrange("p g q j -> p (g q j)"),
+                )
 
         out_sb = {}
         for h in range(2):
@@ -172,7 +231,7 @@ def tile_lokrlayer_kernel(tc, x, original_weight, lokr_A, lokr_B, scalar, out):
                 out_sb[(h, mt)] = opool.tile([P, 64, 16], F32, name="out_sb%d%d" % (h, mt))
 
         def multiply_chunk(c):
-            h, q0, nq = CHUNKS[c]
+            nq = chunks[c][2]
             codes, scales = chunk_tiles[c][1], chunk_tiles[c][2]
             accs = []
             for mt in range(2):
@@ -190,41 +249,51 @@ def tile_lokrlayer_kernel(tc, x, original_weight, lokr_A, lokr_B, scalar, out):
                         start=(g == 0),
                         stop=(g == NG - 1),
                     )
+            return accs
+
+        def copy_out(c, accs):
+            h, q0, nq = chunks[c][0], chunks[c][1], chunks[c][2]
             for mt in range(2):
-                dst = out_sb[(h, mt)][:, :, q0:q0 + nq]
-                src = accs[mt][:].rearrange("m (q r) -> m r q", q=nq)
-                nc.scalar.copy(out=dst, in_=src)
-            if q0 + nq == 16:
-                for mt in range(2):
+                nc.scalar.copy(
+                    out=out_sb[(h, mt)][:, :, q0:q0 + nq],
+                    in_=accs[mt][:].rearrange("m (q r) -> m r q", q=nq),
+                )
+                if q0 + nq == 16:
                     nc.sync.dma_start(
                         out=out[mt * P:(mt + 1) * P, h * 1024:(h + 1) * 1024],
                         in_=out_sb[(h, mt)][:].rearrange("m r q -> m (r q)"),
                     )
 
-        n_units = 32
-        after = {}
-        for i in range(n_units):
-            after[i] = []
-        after[5].append(transpose_x)
-        after[10].append(quantise_x)
-        for c, (h, q0, nq) in enumerate(CHUNKS):
-            end = h * 16 + q0 + nq - 1
-            parts = 2 if nq == 8 else 1
-            for part in range(parts):
-                at_unit = min(end + 2 * (part + 1), n_units - 1)
-                after[at_unit].append((c, part, parts))
-
-        for i in range(LOOKAHEAD):
-            transpose_unit(i)
-        for i in range(n_units):
-            if i + LOOKAHEAD < n_units:
-                transpose_unit(i + LOOKAHEAD)
-            combine_unit(i)
-            for job in after[i]:
-                if isinstance(job, tuple):
-                    c, part, parts = job
-                    quantise_chunk(c, part, parts)
-                    if part == parts - 1:
-                        multiply_chunk(c)
+        late = []
+        transpose_ready_units()
+        stage_for_pool(0)
+        copy_at(0, 1)
+        copy_at(1, 1)
+        transpose_ready_units()
+        for i in range(N_UNITS):
+            ahead = i + STAGE_AHEAD
+            if ahead < N_UNITS and on_pool[ahead]:
+                stage_for_pool(ahead)
+                transpose_ready_units()
+            if on_pool[i]:
+                combine_on_pool(i)
+            else:
+                combine_on_vector(i)
+                transpose_ready_units()
+            if i == X_TRANSPOSE_AFTER:
+                transpose_x()
+            if i == LATE_COPY_AFTER:
+                for (c, accs) in late:
+                    copy_out(c, accs)
+            if i in phase_end:
+                cs = [c for c in range(len(chunks)) if chunk_of[i][0] - len(phase_end[i]) < c <= chunk_of[i][0]]
+                if i == X_TRANSPOSE_AFTER:
+                    quantise_chunk(cs[0])
+                    quantise_x()
+                    copy_out(cs[0], multiply_chunk(cs[0]))
+                    quantise_chunk(cs[1])
+                    late.append((cs[1], multiply_chunk(cs[1])))
                 else:
-                    job()
+                    for c in cs:
+                        quantise_chunk(c)
+                        copy_out(c, multiply_chunk(c))

@@ -17,18 +17,17 @@ P = 128
 NG = 4
 N_UNITS = 32
 TP_BANKS = 6
-W_PIECES = [(0, 0, 1), (0, 1, 1), (0, 2, 2), (0, 4, 2), (0, 6, 2), (0, 8, 4), (0, 12, 4),
+W_PIECES = [(0, 0, 1), (0, 1, 1), (0, 2, 2), (0, 4, 2), (0, 6, 2), (0, 8, 2), (0, 10, 2), (0, 12, 4),
             (1, 0, 4), (1, 4, 4), (1, 8, 4), (1, 12, 4)]
-X_AFTER_PIECE = 6
+X_AFTER_PIECE = 4
 PHASES = [
-    [(0, 0, 8, "ga"), (0, 8, 8, "gb")],
-    [(1, 0, 8, "gb"), (1, 8, 4, "ga")],
-    [(1, 12, 4, "ga")],
+    [(0, 0, 8, "g")],
+    [(0, 8, 8, "g")],
+    [(1, 0, 8, "g")],
+    [(1, 8, 8, "g")],
 ]
-ROUND = 3
-STAGE_AHEAD = 3
-X_TRANSPOSE_AFTER = 15
-LATE_COPY_AFTER = 19
+ROUND = 4
+X_TRANSPOSE_AFTER = 7
 
 
 def tile_lokrlayer_kernel(tc, x, original_weight, lokr_A, lokr_B, scalar, out):
@@ -168,6 +167,8 @@ def tile_lokrlayer_kernel(tc, x, original_weight, lokr_A, lokr_B, scalar, out):
                     )
                 banks[i] = bank
                 state["next"] = i + 1
+                if on_pool[i]:
+                    stage_for_pool(i)
 
         def grouped_slice(i):
             c, ql = chunk_of[i]
@@ -264,17 +265,10 @@ def tile_lokrlayer_kernel(tc, x, original_weight, lokr_A, lokr_B, scalar, out):
                         in_=out_sb[(h, mt)][:].rearrange("m r q -> m (r q)"),
                     )
 
-        late = []
         transpose_ready_units()
-        stage_for_pool(0)
         copy_at(0, 1)
         copy_at(1, 1)
-        transpose_ready_units()
         for i in range(N_UNITS):
-            ahead = i + STAGE_AHEAD
-            if ahead < N_UNITS and on_pool[ahead]:
-                stage_for_pool(ahead)
-                transpose_ready_units()
             if on_pool[i]:
                 combine_on_pool(i)
             else:
@@ -282,18 +276,15 @@ def tile_lokrlayer_kernel(tc, x, original_weight, lokr_A, lokr_B, scalar, out):
                 transpose_ready_units()
             if i == X_TRANSPOSE_AFTER:
                 transpose_x()
-            if i == LATE_COPY_AFTER:
-                for (c, accs) in late:
-                    copy_out(c, accs)
             if i in phase_end:
-                cs = [c for c in range(len(chunks)) if chunk_of[i][0] - len(phase_end[i]) < c <= chunk_of[i][0]]
-                if i == X_TRANSPOSE_AFTER:
-                    quantise_chunk(cs[0])
+                c = chunk_of[i][0]
+                if c == 0:
+                    quantise_chunk(0)
+                elif c == 1:
                     quantise_x()
-                    copy_out(cs[0], multiply_chunk(cs[0]))
-                    quantise_chunk(cs[1])
-                    late.append((cs[1], multiply_chunk(cs[1])))
+                    copy_out(0, multiply_chunk(0))
+                    quantise_chunk(1)
+                    copy_out(1, multiply_chunk(1))
                 else:
-                    for c in cs:
-                        quantise_chunk(c)
-                        copy_out(c, multiply_chunk(c))
+                    quantise_chunk(c)
+                    copy_out(c, multiply_chunk(c))

@@ -144,7 +144,7 @@ def tile_lokrlayer_kernel(tc, x, original_weight, lokr_A, lokr_B, scalar, out):
                     units.append(h * 16 + q0 + ql)
                 chunks.append((h, q0, nq, tag))
             for idx, i in enumerate(units):
-                on_pool[i] = idx % ROUND == 0 and idx + ROUND <= len(units)
+                on_pool[i] = idx % ROUND == 0 and idx + ROUND <= len(units) and i != 4
             phase_end[units[-1]] = phase
         chunk_tiles = [None for c in chunks]
 
@@ -216,7 +216,7 @@ def tile_lokrlayer_kernel(tc, x, original_weight, lokr_A, lokr_B, scalar, out):
 
         def quantise_chunk(c):
             grouped, codes, scales = chunk_tiles[c]
-            parts = 2 if chunks[c][2] == 8 else 1
+            parts = 4 if c == len(chunks) - 1 else 2
             n = NG // parts
             for part in range(parts):
                 g0 = part * n
@@ -255,10 +255,12 @@ def tile_lokrlayer_kernel(tc, x, original_weight, lokr_A, lokr_B, scalar, out):
         def copy_out(c, accs):
             h, q0, nq = chunks[c][0], chunks[c][1], chunks[c][2]
             for mt in range(2):
-                nc.scalar.copy(
-                    out=out_sb[(h, mt)][:, :, q0:q0 + nq],
-                    in_=accs[mt][:].rearrange("m (q r) -> m r q", q=nq),
-                )
+                dst = out_sb[(h, mt)][:, :, q0:q0 + nq]
+                src = accs[mt][:].rearrange("m (q r) -> m r q", q=nq)
+                if c == len(chunks) - 1 and mt == 1:
+                    nc.vector.tensor_copy(out=dst, in_=src)
+                else:
+                    nc.scalar.copy(out=dst, in_=src)
                 if q0 + nq == 16:
                     nc.sync.dma_start(
                         out=out[mt * P:(mt + 1) * P, h * 1024:(h + 1) * 1024],

@@ -15,19 +15,14 @@ FLOPS = 2 * 256 * 2048 * 2048
 
 P = 128
 NG = 4
+NQ = 16
 N_UNITS = 32
+CHUNK = 8
 TP_BANKS = 6
-W_PIECES = [(0, 0, 1), (0, 1, 1), (0, 2, 2), (0, 4, 2), (0, 6, 2), (0, 8, 2), (0, 10, 2), (0, 12, 4),
-            (1, 0, 4), (1, 4, 4), (1, 8, 4), (1, 12, 4)]
-X_AFTER_PIECE = 4
-PHASES = [
-    [(0, 0, 8, "g")],
-    [(0, 8, 8, "g")],
-    [(1, 0, 8, "g")],
-    [(1, 8, 8, "g")],
-]
-ROUND = 4
-X_TRANSPOSE_AFTER = 7
+W_LOADS = [(0, 1, 2), (1, 1, 2), (2, 2, 2), (4, 4, 5), (8, 4, 5), (12, 4, 5), (16, 4, 5), (20, 4, 5),
+           (24, 4, 5), (28, 2, 2), (30, 2, 2)]
+POOL_EVERY = 4
+POOL_LAST = 24
 
 
 def tile_lokrlayer_kernel(tc, x, original_weight, lokr_A, lokr_B, scalar, out):
@@ -37,48 +32,60 @@ def tile_lokrlayer_kernel(tc, x, original_weight, lokr_A, lokr_B, scalar, out):
         wpool = ctx.enter_context(tc.tile_pool(name="wpool", bufs=1))
         gpool = ctx.enter_context(tc.tile_pool(name="gpool", bufs=1))
         spool = ctx.enter_context(tc.tile_pool(name="spool", bufs=3))
-        cpool = ctx.enter_context(tc.tile_pool(name="cpool", bufs=1))
         opool = ctx.enter_context(tc.tile_pool(name="opool", bufs=1))
         tpp = ctx.enter_context(tc.psum_pool(name="tpp", bufs=TP_BANKS))
-        accp = ctx.enter_context(tc.psum_pool(name="accp", bufs=2))
+        axp = ctx.enter_context(tc.psum_pool(name="axp", bufs=2))
         ctx.enter_context(tc.manual_schedule())
 
         ident = const.tile([P, P], F32, name="ident")
         make_identity(nc, ident[:])
 
-        b_bc = const.tile([P, 16], BF16, name="b_bc")
+        b_bc = const.tile([P, NQ], BF16, name="b_bc")
         nc.scalar.dma_start(out=b_bc[:], in_=lokr_B.rearrange("q o -> (q o)").partition_broadcast(P))
         s_bc = const.tile([P, 1], BF16, name="s_bc")
         nc.scalar.dma_start(out=s_bc[:], in_=scalar.partition_broadcast(P))
-
         a_sb = const.tile([P, 2048], BF16, name="a_sb")
         nc.sync.dma_start(out=a_sb[:], in_=lokr_A)
 
         wv = original_weight.rearrange(
-            "(h r q) (g u j) -> h u r q g j", h=2, r=64, q=16, g=NG, u=2, j=256
+            "(h r q) (g u j) -> h u r q g j", h=2, r=64, q=NQ, g=NG, u=2, j=256
         )
         x_sb = []
         unit_src = {}
-        for n, (h, q0, nq) in enumerate(W_PIECES):
-            wt = wpool.tile([P, nq * 1024], BF16, name="wt%d" % n)
-            for u in range(2):
-                nc.sync.dma_start(
-                    out=wt[u:P:2, :].rearrange("r (q g j) -> r q g j", q=nq, g=NG, j=256),
-                    in_=wv[h, u, :, q0:q0 + nq],
-                )
-            for ql in range(nq):
-                unit_src[h * 16 + q0 + ql] = (wt, ql)
-            if n == X_AFTER_PIECE:
+        progress = {"loads": 0, "transposed": 0, "emptied": 0}
+
+        def start_loads():
+            while progress["loads"] < len(W_LOADS):
+                n = progress["loads"]
+                first, count, slots = W_LOADS[n]
+                same = [m for m in range(n) if W_LOADS[m][1] == count]
+                if len(same) >= slots:
+                    old = W_LOADS[same[len(same) - slots]]
+                    if progress["transposed"] < old[0] + old[1]:
+                        return
+                wt = wpool.tile([P, count * 1024], BF16, name="wt%d" % n, tag="w%d" % count, bufs=slots)
+                h, q0 = first // NQ, first % NQ
+                for u in range(2):
+                    nc.sync.dma_start(
+                        out=wt[u:P:2, :].rearrange("r (q g j) -> r q g j", q=count, g=NG, j=256),
+                        in_=wv[h, u, :, q0:q0 + count],
+                    )
+                for k in range(count):
+                    unit_src[first + k] = (wt, k)
+                progress["loads"] = n + 1
+            if len(x_sb) == 0:
                 for mt in range(2):
                     xt = const.tile([P, 2048], BF16, name="x_sb%d" % mt)
                     nc.sync.dma_start(out=xt[:], in_=x[mt * P:(mt + 1) * P, :])
                     x_sb.append(xt)
 
+        start_loads()
+
         s32 = const.tile([P, 1], F32, name="s32")
         nc.vector.tensor_copy(out=s32[:], in_=s_bc[:])
-        cb = const.tile([P, 16], F32, name="cb")
+        gain = const.tile([P, NQ], F32, name="gain")
         nc.vector.tensor_scalar(
-            out=cb[:], in0=b_bc[:], scalar1=s32[:, 0:1], scalar2=2.0, op0=ALU.mult, op1=ALU.mult
+            out=gain[:], in0=b_bc[:], scalar1=s32[:, 0:1], scalar2=2.0, op0=ALU.mult, op1=ALU.mult
         )
 
         at = const.tile([P, 2048], BF16, name="at")
@@ -86,7 +93,7 @@ def tile_lokrlayer_kernel(tc, x, original_weight, lokr_A, lokr_B, scalar, out):
         a_w = a_sb[:].bitcast(F32)
         pas = []
         for b in range(2):
-            pa = accp.tile([P, 512], F32, name="pa%d" % b, tag="acc")
+            pa = axp.tile([P, 512], F32, name="pa%d" % b, tag="ax")
             for g2 in range(2):
                 for u in range(2):
                     w0 = 256 * (2 * b + g2) + 128 * u
@@ -105,188 +112,131 @@ def tile_lokrlayer_kernel(tc, x, original_weight, lokr_A, lokr_B, scalar, out):
 
         copy_at(0, 0)
         copy_at(1, 0)
-        at_v = at[:].rearrange("p (h g j) -> p h g j", h=2, g=NG, j=256)
+
+        grouped = []
+        codes = []
+        scales = []
+        for c in range(N_UNITS // CHUNK):
+            grouped.append(gpool.tile([P, NG, CHUNK, 256], BF16, name="grouped%d" % c, align_bytes=64))
+            codes.append(gpool.tile([P, NG, CHUNK * 64], U32, name="codes%d" % c, align_bytes=64))
+            scales.append(gpool.tile([P, NG, CHUNK * 64], U8, name="scales%d" % c, align_bytes=64))
+
+        def on_pool(i):
+            return i % POOL_EVERY == 0 and i <= POOL_LAST
+
+        banks = {}
+        staged = {}
+
+        def stage_for_pool(i):
+            h, q = i // NQ, i % NQ
+            delta = spool.tile([P, 1024], F32, name="delta%d" % i, tag="delta")
+            nc.scalar.activation(
+                out=delta[:], in_=at[:, h * 1024:(h + 1) * 1024], func=ACT.Copy, scale=gain[:, q:q + 1]
+            )
+            wts = spool.tile([P, 512], F32, name="wts%d" % i, tag="wts")
+            nc.scalar.copy(out=wts[:], in_=banks[i][:])
+            staged[i] = (wts, delta)
+            progress["emptied"] += 1
+
+        def transpose_units():
+            while progress["transposed"] < N_UNITS and progress["transposed"] - progress["emptied"] < TP_BANKS:
+                i = progress["transposed"]
+                wt, k = unit_src[i]
+                ww = wt[:].bitcast(F32)
+                bank = tpp.tile([P, 512], F32, name="tp%d" % i, tag="tp")
+                for g in range(NG):
+                    w0 = (k * NG + g) * P
+                    nc.tensor.transpose(
+                        out=bank[:, g * P:(g + 1) * P], in_=ww[:, w0:w0 + P], identity=ident[:]
+                    )
+                banks[i] = bank
+                progress["transposed"] = i + 1
+                start_loads()
+                if on_pool(i):
+                    stage_for_pool(i)
+
+        transpose_units()
+        copy_at(0, 1)
+        copy_at(1, 1)
+        for i in range(N_UNITS):
+            h, q = i // NQ, i % NQ
+            dst = grouped[i // CHUNK][:, :, i % CHUNK, :]
+            if on_pool(i):
+                wts, delta = staged[i]
+                nc.gpsimd.tensor_tensor(
+                    out=dst,
+                    in0=wts[:].bitcast(BF16).rearrange("p (g j) -> p g j", g=NG),
+                    in1=delta[:].rearrange("p (g j) -> p g j", g=NG),
+                    op=ALU.add,
+                )
+            else:
+                nc.vector.scalar_tensor_tensor(
+                    out=dst,
+                    in0=at[:, h * 1024:(h + 1) * 1024].rearrange("p (g j) -> p g j", g=NG),
+                    scalar=gain[:, q:q + 1],
+                    in1=banks[i][:].bitcast(BF16).rearrange("p (g j) -> p g j", g=NG),
+                    op0=ALU.mult,
+                    op1=ALU.add,
+                )
+                progress["emptied"] += 1
+                transpose_units()
 
         xg = const.tile([P, 4096], BF16, name="xg", align_bytes=64)
         xg_w = xg[:].bitcast(F32)
         x_codes = const.tile([P, 1024], U32, name="x_codes", align_bytes=64)
         x_scales = const.tile([P, 1024], U8, name="x_scales", align_bytes=64)
-
-        def transpose_x():
-            for g in range(NG):
-                px = accp.tile([P, 512], F32, name="px%d" % g, tag="acc")
-                for u in range(2):
-                    for mt in range(2):
-                        w0 = 256 * g + 128 * u
-                        c0 = (u * 2 + mt) * P
-                        nc.tensor.transpose(
-                            out=px[:, c0:c0 + P],
-                            in_=x_sb[mt][:].bitcast(F32)[:, w0:w0 + P],
-                            identity=ident[:],
-                        )
-                nc.scalar.copy(
-                    out=xg_w[:, g * 512:(g + 1) * 512].rearrange("p (c u) -> p c u", u=2),
-                    in_=px[:].rearrange("p (u c) -> p c u", u=2),
-                )
-
-        def quantise_x():
-            nc.vector.quantize_mx(out=x_codes[:].bitcast(FP8X4), scales=x_scales[:], in_=xg[:])
-
-        chunk_of = {}
-        chunks = []
-        on_pool = {}
-        phase_end = {}
-        for phase in PHASES:
-            units = []
-            for (h, q0, nq, tag) in phase:
-                for ql in range(nq):
-                    chunk_of[h * 16 + q0 + ql] = (len(chunks), ql)
-                    units.append(h * 16 + q0 + ql)
-                chunks.append((h, q0, nq, tag))
-            for idx, i in enumerate(units):
-                on_pool[i] = idx % ROUND == 0 and idx + ROUND <= len(units) and i != 4
-            phase_end[units[-1]] = phase
-        chunk_tiles = [None for c in chunks]
-
-        banks = {}
-        used = {}
-        state = {"next": 0}
-
-        def transpose_ready_units():
-            while state["next"] < N_UNITS and (
-                state["next"] < TP_BANKS or used.get(state["next"] - TP_BANKS, False)
-            ):
-                i = state["next"]
-                wt, ql = unit_src[i]
-                ww = wt[:].bitcast(F32)
-                bank = tpp.tile([P, 512], F32, name="tp%d" % i, tag="tp")
-                for g in range(NG):
-                    w0 = (ql * NG + g) * P
+        for g in range(NG):
+            px = axp.tile([P, 512], F32, name="px%d" % g, tag="ax")
+            for u in range(2):
+                for mt in range(2):
+                    w0 = 256 * g + 128 * u
+                    c0 = (u * 2 + mt) * P
                     nc.tensor.transpose(
-                        out=bank[:, g * P:(g + 1) * P], in_=ww[:, w0:w0 + P], identity=ident[:]
+                        out=px[:, c0:c0 + P], in_=x_sb[mt][:].bitcast(F32)[:, w0:w0 + P], identity=ident[:]
                     )
-                banks[i] = bank
-                state["next"] = i + 1
-                if on_pool[i]:
-                    stage_for_pool(i)
-
-        def grouped_slice(i):
-            c, ql = chunk_of[i]
-            if chunk_tiles[c] is None:
-                nq, tag = chunks[c][2], chunks[c][3]
-                grouped = gpool.tile([P, NG, nq, 256], BF16, name="grouped%d" % c, tag=tag, align_bytes=64)
-                codes = cpool.tile([P, NG, nq * 64], U32, name="codes%d" % c, align_bytes=64)
-                scales = cpool.tile([P, NG, nq * 64], U8, name="scales%d" % c, align_bytes=64)
-                chunk_tiles[c] = (grouped, codes, scales)
-            return chunk_tiles[c][0][:, :, ql, :]
-
-        def combine_on_vector(i):
-            h, q = i // 16, i % 16
-            nc.vector.scalar_tensor_tensor(
-                out=grouped_slice(i),
-                in0=at_v[:, h],
-                scalar=cb[:, q:q + 1],
-                in1=banks[i][:].bitcast(BF16).rearrange("p (g j) -> p g j", g=NG),
-                op0=ALU.mult,
-                op1=ALU.add,
+            nc.scalar.copy(
+                out=xg_w[:, g * 512:(g + 1) * 512].rearrange("p (c u) -> p c u", u=2),
+                in_=px[:].rearrange("p (u c) -> p c u", u=2),
             )
-            used[i] = True
+        nc.vector.quantize_mx(out=x_codes[:].bitcast(FP8X4), scales=x_scales[:], in_=xg[:])
 
-        staged = {}
-
-        def stage_for_pool(i):
-            h, q = i // 16, i % 16
-            delta = spool.tile([P, 1024], F32, name="delta%d" % i, tag="delta")
-            nc.scalar.activation(
-                out=delta[:], in_=at[:, h * 1024:(h + 1) * 1024], func=ACT.Copy, scale=cb[:, q:q + 1]
-            )
-            wts = spool.tile([P, 512], F32, name="wts%d" % i, tag="wts")
-            nc.scalar.copy(out=wts[:], in_=banks[i][:])
-            staged[i] = (wts, delta)
-            used[i] = True
-
-        def combine_on_pool(i):
-            wts, delta = staged[i]
-            nc.gpsimd.tensor_tensor(
-                out=grouped_slice(i),
-                in0=wts[:].bitcast(BF16).rearrange("p (g j) -> p g j", g=NG),
-                in1=delta[:].rearrange("p (g j) -> p g j", g=NG),
-                op=ALU.add,
-            )
-
-        def quantise_chunk(c):
-            grouped, codes, scales = chunk_tiles[c]
-            parts = 4 if c == len(chunks) - 1 else 2
-            n = NG // parts
-            for part in range(parts):
-                g0 = part * n
-                nc.vector.quantize_mx(
-                    out=codes[:, g0:g0 + n, :].rearrange("p g n -> p (g n)").bitcast(FP8X4),
-                    scales=scales[:, g0:g0 + n, :].rearrange("p g n -> p (g n)"),
-                    in_=grouped[:, g0:g0 + n, :, :].rearrange("p g q j -> p (g q j)"),
-                )
-
-        out_sb = {}
-        for h in range(2):
-            for mt in range(2):
-                out_sb[(h, mt)] = opool.tile([P, 64, 16], F32, name="out_sb%d%d" % (h, mt))
-
-        def multiply_chunk(c):
-            nq = chunks[c][2]
-            codes, scales = chunk_tiles[c][1], chunk_tiles[c][2]
+        n_chunks = N_UNITS // CHUNK
+        for c in range(n_chunks):
+            h, q0 = (c * CHUNK) // NQ, (c * CHUNK) % NQ
             accs = []
             for mt in range(2):
-                acc = accp.tile([P, nq * 64], F32, name="acc%d_%d" % (c, mt), tag="acc")
+                acc = tpp.tile([P, CHUNK * 64], F32, name="acc%d_%d" % (c, mt), tag="tp")
                 accs.append(acc)
             for g in range(NG):
+                nc.vector.quantize_mx(
+                    out=codes[c][:, g, :].bitcast(FP8X4),
+                    scales=scales[c][:, g, :],
+                    in_=grouped[c][:, g, :, :].rearrange("p q j -> p (q j)"),
+                )
                 for mt in range(2):
                     m0 = g * 256 + mt * P
                     nc.tensor.matmul_mx(
                         out=accs[mt][:],
                         lhsT=x_codes[:, m0:m0 + P].bitcast(FP8X4),
                         lhsT_scale=x_scales[:, m0:m0 + P],
-                        rhs=codes[:, g, :].bitcast(FP8X4),
-                        rhs_scale=scales[:, g, :],
+                        rhs=codes[c][:, g, :].bitcast(FP8X4),
+                        rhs_scale=scales[c][:, g, :],
                         start=(g == 0),
                         stop=(g == NG - 1),
                     )
-            return accs
-
-        def copy_out(c, accs):
-            h, q0, nq = chunks[c][0], chunks[c][1], chunks[c][2]
             for mt in range(2):
-                dst = out_sb[(h, mt)][:, :, q0:q0 + nq]
-                src = accs[mt][:].rearrange("m (q r) -> m r q", q=nq)
-                if c == len(chunks) - 1 and mt == 1:
+                if q0 == 0:
+                    out_sb = opool.tile([P, 64, NQ], F32, name="out_sb%d%d" % (h, mt))
+                    banks[("out", h, mt)] = out_sb
+                out_sb = banks[("out", h, mt)]
+                dst = out_sb[:, :, q0:q0 + CHUNK]
+                src = accs[mt][:].rearrange("m (q r) -> m r q", q=CHUNK)
+                if c == n_chunks - 1 and mt == 1:
                     nc.vector.tensor_copy(out=dst, in_=src)
                 else:
                     nc.scalar.copy(out=dst, in_=src)
-                if q0 + nq == 16:
+                if q0 + CHUNK == NQ:
                     nc.sync.dma_start(
                         out=out[mt * P:(mt + 1) * P, h * 1024:(h + 1) * 1024],
-                        in_=out_sb[(h, mt)][:].rearrange("m r q -> m (r q)"),
+                        in_=out_sb[:].rearrange("m r q -> m (r q)"),
                     )
-
-        transpose_ready_units()
-        copy_at(0, 1)
-        copy_at(1, 1)
-        for i in range(N_UNITS):
-            if on_pool[i]:
-                combine_on_pool(i)
-            else:
-                combine_on_vector(i)
-                transpose_ready_units()
-            if i == X_TRANSPOSE_AFTER:
-                transpose_x()
-            if i in phase_end:
-                c = chunk_of[i][0]
-                if c == 0:
-                    quantise_chunk(0)
-                elif c == 1:
-                    quantise_x()
-                    copy_out(0, multiply_chunk(0))
-                    quantise_chunk(1)
-                    copy_out(1, multiply_chunk(1))
-                else:
-                    quantise_chunk(c)
-                    copy_out(c, multiply_chunk(c))

@@ -21,8 +21,11 @@ CHUNK = 8
 TP_BANKS = 6
 W_LOADS = [(0, 1, 2), (1, 1, 2), (2, 2, 2), (4, 4, 5), (8, 4, 5), (12, 4, 5), (16, 4, 5), (20, 4, 5),
            (24, 4, 5), (28, 2, 2), (30, 2, 2)]
+X_BEFORE_LOAD = 9
+X_AFTER_UNIT = 27
 POOL_EVERY = 4
-POOL_LAST = 24
+POOL_LAST = 25
+LATE_UNITS = 2
 
 
 def tile_lokrlayer_kernel(tc, x, original_weight, lokr_A, lokr_B, scalar, out):
@@ -45,7 +48,8 @@ def tile_lokrlayer_kernel(tc, x, original_weight, lokr_A, lokr_B, scalar, out):
         s_bc = const.tile([P, 1], BF16, name="s_bc")
         nc.scalar.dma_start(out=s_bc[:], in_=scalar.partition_broadcast(P))
         a_sb = const.tile([P, 2048], BF16, name="a_sb")
-        nc.sync.dma_start(out=a_sb[:], in_=lokr_A)
+        for b in range(2):
+            nc.sync.dma_start(out=a_sb[:, b * 1024:(b + 1) * 1024], in_=lokr_A[:, b * 1024:(b + 1) * 1024])
 
         wv = original_weight.rearrange(
             "(h r q) (g u j) -> h u r q g j", h=2, r=64, q=NQ, g=NG, u=2, j=256
@@ -57,6 +61,11 @@ def tile_lokrlayer_kernel(tc, x, original_weight, lokr_A, lokr_B, scalar, out):
         def start_loads():
             while progress["loads"] < len(W_LOADS):
                 n = progress["loads"]
+                if n == X_BEFORE_LOAD and len(x_sb) == 0:
+                    for mt in range(2):
+                        xt = const.tile([P, 2048], BF16, name="x_sb%d" % mt)
+                        nc.sync.dma_start(out=xt[:], in_=x[mt * P:(mt + 1) * P, :])
+                        x_sb.append(xt)
                 first, count, slots = W_LOADS[n]
                 same = [m for m in range(n) if W_LOADS[m][1] == count]
                 if len(same) >= slots:
@@ -73,11 +82,6 @@ def tile_lokrlayer_kernel(tc, x, original_weight, lokr_A, lokr_B, scalar, out):
                 for k in range(count):
                     unit_src[first + k] = (wt, k)
                 progress["loads"] = n + 1
-            if len(x_sb) == 0:
-                for mt in range(2):
-                    xt = const.tile([P, 2048], BF16, name="x_sb%d" % mt)
-                    nc.sync.dma_start(out=xt[:], in_=x[mt * P:(mt + 1) * P, :])
-                    x_sb.append(xt)
 
         start_loads()
 
@@ -122,10 +126,30 @@ def tile_lokrlayer_kernel(tc, x, original_weight, lokr_A, lokr_B, scalar, out):
             scales.append(gpool.tile([P, NG, CHUNK * 64], U8, name="scales%d" % c, align_bytes=64))
 
         def on_pool(i):
-            return i % POOL_EVERY == 0 and i <= POOL_LAST
+            return i % POOL_EVERY == 1 and i <= POOL_LAST
 
         banks = {}
         staged = {}
+
+        xg = const.tile([P, 4096], BF16, name="xg", align_bytes=64)
+        xg_w = xg[:].bitcast(F32)
+        x_codes = const.tile([P, 1024], U32, name="x_codes", align_bytes=64)
+        x_scales = const.tile([P, 1024], U8, name="x_scales", align_bytes=64)
+
+        def transpose_x():
+            for g in range(NG):
+                px = axp.tile([P, 512], F32, name="px%d" % g, tag="ax")
+                for u in range(2):
+                    for mt in range(2):
+                        w0 = 256 * g + 128 * u
+                        c0 = (u * 2 + mt) * P
+                        nc.tensor.transpose(
+                            out=px[:, c0:c0 + P], in_=x_sb[mt][:].bitcast(F32)[:, w0:w0 + P], identity=ident[:]
+                        )
+                nc.scalar.copy(
+                    out=xg_w[:, g * 512:(g + 1) * 512].rearrange("p (c u) -> p c u", u=2),
+                    in_=px[:].rearrange("p (u c) -> p c u", u=2),
+                )
 
         def stage_for_pool(i):
             h, q = i // NQ, i % NQ
@@ -154,11 +178,10 @@ def tile_lokrlayer_kernel(tc, x, original_weight, lokr_A, lokr_B, scalar, out):
                 start_loads()
                 if on_pool(i):
                     stage_for_pool(i)
+                if i == X_AFTER_UNIT:
+                    transpose_x()
 
-        transpose_units()
-        copy_at(0, 1)
-        copy_at(1, 1)
-        for i in range(N_UNITS):
+        def combine(i):
             h, q = i // NQ, i % NQ
             dst = grouped[i // CHUNK][:, :, i % CHUNK, :]
             if on_pool(i):
@@ -181,27 +204,9 @@ def tile_lokrlayer_kernel(tc, x, original_weight, lokr_A, lokr_B, scalar, out):
                 progress["emptied"] += 1
                 transpose_units()
 
-        xg = const.tile([P, 4096], BF16, name="xg", align_bytes=64)
-        xg_w = xg[:].bitcast(F32)
-        x_codes = const.tile([P, 1024], U32, name="x_codes", align_bytes=64)
-        x_scales = const.tile([P, 1024], U8, name="x_scales", align_bytes=64)
-        for g in range(NG):
-            px = axp.tile([P, 512], F32, name="px%d" % g, tag="ax")
-            for u in range(2):
-                for mt in range(2):
-                    w0 = 256 * g + 128 * u
-                    c0 = (u * 2 + mt) * P
-                    nc.tensor.transpose(
-                        out=px[:, c0:c0 + P], in_=x_sb[mt][:].bitcast(F32)[:, w0:w0 + P], identity=ident[:]
-                    )
-            nc.scalar.copy(
-                out=xg_w[:, g * 512:(g + 1) * 512].rearrange("p (c u) -> p c u", u=2),
-                in_=px[:].rearrange("p (u c) -> p c u", u=2),
-            )
-        nc.vector.quantize_mx(out=x_codes[:].bitcast(FP8X4), scales=x_scales[:], in_=xg[:])
-
         n_chunks = N_UNITS // CHUNK
-        for c in range(n_chunks):
+
+        def product(c):
             h, q0 = (c * CHUNK) // NQ, (c * CHUNK) % NQ
             accs = []
             for mt in range(2):
@@ -240,3 +245,15 @@ def tile_lokrlayer_kernel(tc, x, original_weight, lokr_A, lokr_B, scalar, out):
                         out=out[mt * P:(mt + 1) * P, h * 1024:(h + 1) * 1024],
                         in_=out_sb[:].rearrange("m r q -> m (r q)"),
                     )
+
+        transpose_units()
+        copy_at(0, 1)
+        copy_at(1, 1)
+        for i in range(N_UNITS - LATE_UNITS):
+            combine(i)
+        nc.vector.quantize_mx(out=x_codes[:].bitcast(FP8X4), scales=x_scales[:], in_=xg[:])
+        product(0)
+        for i in range(N_UNITS - LATE_UNITS, N_UNITS):
+            combine(i)
+        for c in range(1, n_chunks):
+            product(c)

@@ -16,16 +16,24 @@ FLOPS = 2 * 256 * 2048 * 2048
 P = 128
 NG = 4
 NQ = 16
-N_UNITS = 32
 CHUNK = 8
 TP_BANKS = 6
-W_LOADS = [(0, 1, 2), (1, 1, 2), (2, 2, 2), (4, 4, 5), (8, 4, 5), (12, 4, 5), (16, 4, 5), (20, 4, 5),
-           (24, 4, 5), (28, 2, 2), (30, 2, 2)]
-X_BEFORE_LOAD = 9
-X_AFTER_UNIT = 27
-POOL_EVERY = 4
-POOL_LAST = 25
-LATE_UNITS = 2
+
+
+def load_list():
+    loads = []
+    for n in range(8):
+        h, q0 = n // 4, 4 * (n % 4)
+        if n == 7:
+            loads.append(("x",))
+        if n < 2 or n == 7:
+            loads.append(("v", h, q0, 1))
+            loads.append(("v", h, q0 + 1, 2))
+        else:
+            loads.append(("v", h, q0, 3))
+        if n % 2 == 0:
+            loads.append(("p", 2 * n + 3))
+    return loads
 
 
 def tile_lokrlayer_kernel(tc, x, original_weight, lokr_A, lokr_B, scalar, out):
@@ -34,7 +42,7 @@ def tile_lokrlayer_kernel(tc, x, original_weight, lokr_A, lokr_B, scalar, out):
         const = ctx.enter_context(tc.tile_pool(name="const", bufs=1))
         wpool = ctx.enter_context(tc.tile_pool(name="wpool", bufs=1))
         gpool = ctx.enter_context(tc.tile_pool(name="gpool", bufs=1))
-        spool = ctx.enter_context(tc.tile_pool(name="spool", bufs=3))
+        spool = ctx.enter_context(tc.tile_pool(name="spool", bufs=1))
         opool = ctx.enter_context(tc.tile_pool(name="opool", bufs=1))
         tpp = ctx.enter_context(tc.psum_pool(name="tpp", bufs=TP_BANKS))
         axp = ctx.enter_context(tc.psum_pool(name="axp", bufs=2))
@@ -51,37 +59,40 @@ def tile_lokrlayer_kernel(tc, x, original_weight, lokr_A, lokr_B, scalar, out):
         for b in range(2):
             nc.sync.dma_start(out=a_sb[:, b * 1024:(b + 1) * 1024], in_=lokr_A[:, b * 1024:(b + 1) * 1024])
 
-        wv = original_weight.rearrange(
+        w_pairs = original_weight.rearrange(
             "(h r q) (g u j) -> h u r q g j", h=2, r=64, q=NQ, g=NG, u=2, j=256
         )
-        x_sb = []
-        unit_src = {}
-        progress = {"loads": 0, "transposed": 0, "emptied": 0}
+        w_rows = original_weight.rearrange("(p q) k -> q p k", q=NQ)
+        loads = load_list()
+        slots = {"v1": 2, "v2": 2, "v3": 5, "p": 2, "x": 1}
+        tiles = {}
+        progress = {"loaded": 0, "transposed": 0, "held": 0, "combined": 0}
+
+        def kind(n):
+            return loads[n][0] + ("%d" % loads[n][3] if loads[n][0] == "v" else "")
 
         def start_loads():
-            while progress["loads"] < len(W_LOADS):
-                n = progress["loads"]
-                if n == X_BEFORE_LOAD and len(x_sb) == 0:
-                    for mt in range(2):
-                        xt = const.tile([P, 2048], BF16, name="x_sb%d" % mt)
-                        nc.sync.dma_start(out=xt[:], in_=x[mt * P:(mt + 1) * P, :])
-                        x_sb.append(xt)
-                first, count, slots = W_LOADS[n]
-                same = [m for m in range(n) if W_LOADS[m][1] == count]
-                if len(same) >= slots:
-                    old = W_LOADS[same[len(same) - slots]]
-                    if progress["transposed"] < old[0] + old[1]:
-                        return
-                wt = wpool.tile([P, count * 1024], BF16, name="wt%d" % n, tag="w%d" % count, bufs=slots)
-                h, q0 = first // NQ, first % NQ
-                for u in range(2):
-                    nc.sync.dma_start(
-                        out=wt[u:P:2, :].rearrange("r (q g j) -> r q g j", q=count, g=NG, j=256),
-                        in_=wv[h, u, :, q0:q0 + count],
-                    )
-                for k in range(count):
-                    unit_src[first + k] = (wt, k)
-                progress["loads"] = n + 1
+            while progress["loaded"] < len(loads):
+                n = progress["loaded"]
+                same = [m for m in range(n) if kind(m) == kind(n)]
+                if len(same) >= slots[kind(n)] and progress["transposed"] <= same[len(same) - slots[kind(n)]]:
+                    return
+                if loads[n][0] == "v":
+                    h, q0, count = loads[n][1], loads[n][2], loads[n][3]
+                    wt = wpool.tile([P, count * 1024], BF16, name="wt%d" % n, tag=kind(n), bufs=slots[kind(n)])
+                    for u in range(2):
+                        nc.sync.dma_start(
+                            out=wt[u:P:2, :].rearrange("r (q g j) -> r q g j", q=count, g=NG, j=256),
+                            in_=w_pairs[h, u, :, q0:q0 + count],
+                        )
+                elif loads[n][0] == "p":
+                    wt = wpool.tile([P, 2048], BF16, name="wt%d" % n, tag="p", bufs=slots["p"])
+                    nc.sync.dma_start(out=wt[:], in_=w_rows[loads[n][1]])
+                else:
+                    wt = wpool.tile([P, 2, 2048], BF16, name="x_sb")
+                    nc.sync.dma_start(out=wt[:], in_=x.rearrange("(t m) k -> m t k", t=2))
+                tiles[n] = wt
+                progress["loaded"] = n + 1
 
         start_loads()
 
@@ -92,125 +103,129 @@ def tile_lokrlayer_kernel(tc, x, original_weight, lokr_A, lokr_B, scalar, out):
             out=gain[:], in0=b_bc[:], scalar1=s32[:, 0:1], scalar2=2.0, op0=ALU.mult, op1=ALU.mult
         )
 
-        at = const.tile([P, 2048], BF16, name="at")
-        at_w = at[:].bitcast(F32)
-        a_w = a_sb[:].bitcast(F32)
-        pas = []
-        for b in range(2):
-            pa = axp.tile([P, 512], F32, name="pa%d" % b, tag="ax")
+        def transpose_planes(bank, words, b):
             for g2 in range(2):
                 for u in range(2):
                     w0 = 256 * (2 * b + g2) + 128 * u
                     c0 = (g2 * 2 + u) * P
-                    nc.tensor.transpose(out=pa[:, c0:c0 + P], in_=a_w[:, w0:w0 + P], identity=ident[:])
+                    nc.tensor.transpose(out=bank[:, c0:c0 + P], in_=words[:, w0:w0 + P], identity=ident[:])
+
+        def pair_up(bank, h):
+            return bank[:].rearrange("p (g u h r) -> p h g r u", g=2, u=2, h=2, r=64)[:, h]
+
+        def paired(words, b):
+            return words[:, 2 * b * P:2 * (b + 1) * P].rearrange("p (g r u) -> p g r u", g=2, r=64, u=2)
+
+        at = [const.tile([P, 1024], BF16, name="at%d" % h) for h in range(2)]
+        pas = []
+        for b in range(2):
+            pa = axp.tile([P, 512], F32, name="pa%d" % b, tag="ax")
+            transpose_planes(pa, a_sb[:].bitcast(F32), b)
             pas.append(pa)
+        for h in range(2):
+            nc.scalar.copy(out=paired(at[h][:].bitcast(F32), 0), in_=pair_up(pas[0], h))
+            nc.vector.tensor_copy(out=paired(at[h][:].bitcast(F32), 1), in_=pair_up(pas[1], h))
 
-        def copy_at(b, h):
-            src = pas[b][:].rearrange("p (g u h r) -> p h g r u", g=2, u=2, h=2, r=64)
-            d0 = (h * NG + 2 * b) * P
-            dst = at_w[:, d0:d0 + 2 * P].rearrange("p (g r u) -> p g r u", g=2, r=64, u=2)
-            if b == 0:
-                nc.scalar.copy(out=dst, in_=src[:, h])
-            else:
-                nc.vector.tensor_copy(out=dst, in_=src[:, h])
-
-        copy_at(0, 0)
-        copy_at(1, 0)
-
+        n_chunks = 2 * NQ // CHUNK
         grouped = []
         codes = []
         scales = []
-        for c in range(N_UNITS // CHUNK):
+        for c in range(n_chunks):
             grouped.append(gpool.tile([P, NG, CHUNK, 256], BF16, name="grouped%d" % c, align_bytes=64))
             codes.append(gpool.tile([P, NG, CHUNK * 64], U32, name="codes%d" % c, align_bytes=64))
             scales.append(gpool.tile([P, NG, CHUNK * 64], U8, name="scales%d" % c, align_bytes=64))
 
-        def on_pool(i):
-            return i % POOL_EVERY == 1 and i <= POOL_LAST
-
-        banks = {}
-        staged = {}
+        def grouped_slice(h, q):
+            return grouped[(h * NQ + q) // CHUNK][:, :, q % CHUNK, :]
 
         xg = const.tile([P, 4096], BF16, name="xg", align_bytes=64)
-        xg_w = xg[:].bitcast(F32)
         x_codes = const.tile([P, 1024], U32, name="x_codes", align_bytes=64)
         x_scales = const.tile([P, 1024], U8, name="x_scales", align_bytes=64)
 
-        def transpose_x():
+        def transpose_x(x_sb):
             for g in range(NG):
                 px = axp.tile([P, 512], F32, name="px%d" % g, tag="ax")
                 for u in range(2):
-                    for mt in range(2):
+                    for t in range(2):
                         w0 = 256 * g + 128 * u
-                        c0 = (u * 2 + mt) * P
+                        c0 = (u * 2 + t) * P
                         nc.tensor.transpose(
-                            out=px[:, c0:c0 + P], in_=x_sb[mt][:].bitcast(F32)[:, w0:w0 + P], identity=ident[:]
+                            out=px[:, c0:c0 + P], in_=x_sb[:, t, :].bitcast(F32)[:, w0:w0 + P], identity=ident[:]
                         )
                 nc.scalar.copy(
-                    out=xg_w[:, g * 512:(g + 1) * 512].rearrange("p (c u) -> p c u", u=2),
+                    out=xg[:].bitcast(F32)[:, g * 512:(g + 1) * 512].rearrange("p (c u) -> p c u", u=2),
                     in_=px[:].rearrange("p (u c) -> p c u", u=2),
                 )
 
-        def stage_for_pool(i):
-            h, q = i // NQ, i % NQ
-            delta = spool.tile([P, 1024], F32, name="delta%d" % i, tag="delta")
-            nc.scalar.activation(
-                out=delta[:], in_=at[:, h * 1024:(h + 1) * 1024], func=ACT.Copy, scale=gain[:, q:q + 1]
-            )
-            wts = spool.tile([P, 512], F32, name="wts%d" % i, tag="wts")
-            nc.scalar.copy(out=wts[:], in_=banks[i][:])
-            staged[i] = (wts, delta)
-            progress["emptied"] += 1
-
-        def transpose_units():
-            while progress["transposed"] < N_UNITS and progress["transposed"] - progress["emptied"] < TP_BANKS:
-                i = progress["transposed"]
-                wt, k = unit_src[i]
-                ww = wt[:].bitcast(F32)
-                bank = tpp.tile([P, 512], F32, name="tp%d" % i, tag="tp")
-                for g in range(NG):
-                    w0 = (k * NG + g) * P
-                    nc.tensor.transpose(
-                        out=bank[:, g * P:(g + 1) * P], in_=ww[:, w0:w0 + P], identity=ident[:]
-                    )
-                banks[i] = bank
-                progress["transposed"] = i + 1
-                start_loads()
-                if on_pool(i):
-                    stage_for_pool(i)
-                if i == X_AFTER_UNIT:
-                    transpose_x()
-
-        def combine(i):
-            h, q = i // NQ, i % NQ
-            dst = grouped[i // CHUNK][:, :, i % CHUNK, :]
-            if on_pool(i):
-                wts, delta = staged[i]
+        def combine_on_pool(q, wt):
+            pq = []
+            for b in range(2):
+                bank = tpp.tile([P, 512], F32, name="pq%d_%d" % (q, b), tag="tp")
+                transpose_planes(bank, wt[:].bitcast(F32), b)
+                pq.append(bank)
+            for h in range(2):
+                delta = spool.tile([P, 1024], F32, name="delta%d_%d" % (q, h), tag="delta", bufs=3)
+                nc.scalar.activation(out=delta[:], in_=at[h][:], func=ACT.Copy, scale=gain[:, q:q + 1])
+                wts = spool.tile([P, 512], F32, name="wts%d_%d" % (q, h), tag="wts", bufs=4)
+                for b in range(2):
+                    nc.scalar.copy(out=paired(wts[:], b), in_=pair_up(pq[b], h))
                 nc.gpsimd.tensor_tensor(
-                    out=dst,
+                    out=grouped_slice(h, q),
                     in0=wts[:].bitcast(BF16).rearrange("p (g j) -> p g j", g=NG),
                     in1=delta[:].rearrange("p (g j) -> p g j", g=NG),
                     op=ALU.add,
                 )
-            else:
-                nc.vector.scalar_tensor_tensor(
-                    out=dst,
-                    in0=at[:, h * 1024:(h + 1) * 1024].rearrange("p (g j) -> p g j", g=NG),
-                    scalar=gain[:, q:q + 1],
-                    in1=banks[i][:].bitcast(BF16).rearrange("p (g j) -> p g j", g=NG),
-                    op0=ALU.mult,
-                    op1=ALU.add,
-                )
-                progress["emptied"] += 1
-                transpose_units()
 
-        n_chunks = N_UNITS // CHUNK
+        waiting = []
 
-        def product(c):
+        def transpose_ahead():
+            while progress["transposed"] < len(loads):
+                n = progress["transposed"]
+                need = {"v": loads[n][-1], "p": 2, "x": 0}[loads[n][0]]
+                if progress["held"] + need > TP_BANKS:
+                    return
+                if loads[n][0] == "v":
+                    h, q0, count = loads[n][1], loads[n][2], loads[n][3]
+                    for k in range(count):
+                        bank = tpp.tile([P, 512], F32, name="tp%d_%d" % (h, q0 + k), tag="tp")
+                        for g in range(NG):
+                            w0 = (k * NG + g) * P
+                            nc.tensor.transpose(
+                                out=bank[:, g * P:(g + 1) * P],
+                                in_=tiles[n][:].bitcast(F32)[:, w0:w0 + P],
+                                identity=ident[:],
+                            )
+                        waiting.append((h, q0 + k, bank))
+                    progress["held"] += count
+                elif loads[n][0] == "p":
+                    combine_on_pool(loads[n][1], tiles[n])
+                else:
+                    transpose_x(tiles[n])
+                progress["transposed"] = n + 1
+                start_loads()
+
+        transpose_ahead()
+        while progress["combined"] < len(waiting):
+            h, q, bank = waiting[progress["combined"]]
+            progress["combined"] += 1
+            nc.vector.scalar_tensor_tensor(
+                out=grouped_slice(h, q),
+                in0=at[h][:].rearrange("p (g j) -> p g j", g=NG),
+                scalar=gain[:, q:q + 1],
+                in1=bank[:].bitcast(BF16).rearrange("p (g j) -> p g j", g=NG),
+                op0=ALU.mult,
+                op1=ALU.add,
+            )
+            progress["held"] -= 1
+            transpose_ahead()
+
+        nc.vector.quantize_mx(out=x_codes[:].bitcast(FP8X4), scales=x_scales[:], in_=xg[:])
+        out_sb = {}
+        for c in range(n_chunks):
             h, q0 = (c * CHUNK) // NQ, (c * CHUNK) % NQ
             accs = []
-            for mt in range(2):
-                acc = tpp.tile([P, CHUNK * 64], F32, name="acc%d_%d" % (c, mt), tag="tp")
+            for t in range(2):
+                acc = tpp.tile([P, CHUNK * 64], F32, name="acc%d_%d" % (c, t), tag="tp")
                 accs.append(acc)
             for g in range(NG):
                 nc.vector.quantize_mx(
@@ -218,10 +233,10 @@ def tile_lokrlayer_kernel(tc, x, original_weight, lokr_A, lokr_B, scalar, out):
                     scales=scales[c][:, g, :],
                     in_=grouped[c][:, g, :, :].rearrange("p q j -> p (q j)"),
                 )
-                for mt in range(2):
-                    m0 = g * 256 + mt * P
+                for t in range(2):
+                    m0 = g * 256 + t * P
                     nc.tensor.matmul_mx(
-                        out=accs[mt][:],
+                        out=accs[t][:],
                         lhsT=x_codes[:, m0:m0 + P].bitcast(FP8X4),
                         lhsT_scale=x_scales[:, m0:m0 + P],
                         rhs=codes[c][:, g, :].bitcast(FP8X4),
@@ -229,31 +244,17 @@ def tile_lokrlayer_kernel(tc, x, original_weight, lokr_A, lokr_B, scalar, out):
                         start=(g == 0),
                         stop=(g == NG - 1),
                     )
-            for mt in range(2):
+            for t in range(2):
                 if q0 == 0:
-                    out_sb = opool.tile([P, 64, NQ], F32, name="out_sb%d%d" % (h, mt))
-                    banks[("out", h, mt)] = out_sb
-                out_sb = banks[("out", h, mt)]
-                dst = out_sb[:, :, q0:q0 + CHUNK]
-                src = accs[mt][:].rearrange("m (q r) -> m r q", q=CHUNK)
-                if c == n_chunks - 1 and mt == 1:
+                    out_sb[(h, t)] = opool.tile([P, 64, NQ], F32, name="out_sb%d%d" % (h, t))
+                dst = out_sb[(h, t)][:, :, q0:q0 + CHUNK]
+                src = accs[t][:].rearrange("m (q r) -> m r q", q=CHUNK)
+                if c == n_chunks - 1 and t == 1:
                     nc.vector.tensor_copy(out=dst, in_=src)
                 else:
                     nc.scalar.copy(out=dst, in_=src)
                 if q0 + CHUNK == NQ:
                     nc.sync.dma_start(
-                        out=out[mt * P:(mt + 1) * P, h * 1024:(h + 1) * 1024],
-                        in_=out_sb[:].rearrange("m r q -> m (r q)"),
+                        out=out[t * P:(t + 1) * P, h * 1024:(h + 1) * 1024],
+                        in_=out_sb[(h, t)][:].rearrange("m r q -> m (r q)"),
                     )
-
-        transpose_units()
-        copy_at(0, 1)
-        copy_at(1, 1)
-        for i in range(N_UNITS - LATE_UNITS):
-            combine(i)
-        nc.vector.quantize_mx(out=x_codes[:].bitcast(FP8X4), scales=x_scales[:], in_=xg[:])
-        product(0)
-        for i in range(N_UNITS - LATE_UNITS, N_UNITS):
-            combine(i)
-        for c in range(1, n_chunks):
-            product(c)

@@ -28,11 +28,13 @@ def load_list():
             loads.append(("x",))
         if n < 2 or n == 7:
             loads.append(("v", h, q0, 1))
+            if n == 0:
+                loads.append(("p", 3))
             loads.append(("v", h, q0 + 1, 2))
         else:
             loads.append(("v", h, q0, 3))
-        if n % 2 == 0:
-            loads.append(("p", 2 * n + 3))
+            if n % 2 == 0:
+                loads.append(("p", 2 * n + 3))
     return loads
 
 
@@ -219,7 +221,6 @@ def tile_lokrlayer_kernel(tc, x, original_weight, lokr_A, lokr_B, scalar, out):
             progress["held"] -= 1
             transpose_ahead()
 
-        nc.vector.quantize_mx(out=x_codes[:].bitcast(FP8X4), scales=x_scales[:], in_=xg[:])
         out_sb = {}
         for c in range(n_chunks):
             h, q0 = (c * CHUNK) // NQ, (c * CHUNK) % NQ
@@ -228,6 +229,12 @@ def tile_lokrlayer_kernel(tc, x, original_weight, lokr_A, lokr_B, scalar, out):
                 acc = tpp.tile([P, CHUNK * 64], F32, name="acc%d_%d" % (c, t), tag="tp")
                 accs.append(acc)
             for g in range(NG):
+                if c == 0:
+                    nc.vector.quantize_mx(
+                        out=x_codes[:, g * 256:(g + 1) * 256].bitcast(FP8X4),
+                        scales=x_scales[:, g * 256:(g + 1) * 256],
+                        in_=xg[:, g * 1024:(g + 1) * 1024],
+                    )
                 nc.vector.quantize_mx(
                     out=codes[c][:, g, :].bitcast(FP8X4),
                     scales=scales[c][:, g, :],

from contextlib import ExitStack

import concourse.mybir as mybir
from concourse.masks import make_identity

FP8X4 = mybir.dt.float8_e4m3fn_x4
BF16 = mybir.dt.bfloat16
F32 = mybir.dt.float32
U32 = mybir.dt.uint32
U8 = mybir.dt.uint8
ALU = mybir.AluOpType
ACT = mybir.ActivationFunctionType

FLOPS = 2 * 256 * 2048 * 2048

P = 128
NG = 4
NQ = 16
CHUNK = 8
TP_BANKS = 6


def load_list():
    loads = []
    for n in range(8):
        h, q0 = n // 4, 4 * (n % 4)
        if n == 7:
            loads.append(("x",))
        if n < 2 or n == 7:
            loads.append(("v", h, q0, 1))
            if n == 0:
                loads.append(("p", 3))
            loads.append(("v", h, q0 + 1, 2))
        else:
            loads.append(("v", h, q0, 3))
            if n % 2 == 0:
                loads.append(("p", 2 * n + 3))
    return loads


def tile_lokrlayer_kernel(tc, x, original_weight, lokr_A, lokr_B, scalar, out):
    nc = tc.nc
    with ExitStack() as ctx:
        const = ctx.enter_context(tc.tile_pool(name="const", bufs=1))
        wpool = ctx.enter_context(tc.tile_pool(name="wpool", bufs=1))
        gpool = ctx.enter_context(tc.tile_pool(name="gpool", bufs=1))
        spool = ctx.enter_context(tc.tile_pool(name="spool", bufs=1))
        opool = ctx.enter_context(tc.tile_pool(name="opool", bufs=1))
        tpp = ctx.enter_context(tc.psum_pool(name="tpp", bufs=TP_BANKS))
        axp = ctx.enter_context(tc.psum_pool(name="axp", bufs=2))
        ctx.enter_context(tc.manual_schedule())

        ident = const.tile([P, P], F32, name="ident")
        make_identity(nc, ident[:])

        b_bc = const.tile([P, NQ], BF16, name="b_bc")
        nc.scalar.dma_start(out=b_bc[:], in_=lokr_B.rearrange("q o -> (q o)").partition_broadcast(P))
        s_bc = const.tile([P, 1], BF16, name="s_bc")
        nc.scalar.dma_start(out=s_bc[:], in_=scalar.partition_broadcast(P))
        a_sb = const.tile([P, 2048], BF16, name="a_sb")
        for b in range(2):
            nc.sync.dma_start(out=a_sb[:, b * 1024:(b + 1) * 1024], in_=lokr_A[:, b * 1024:(b + 1) * 1024])

        w_pairs = original_weight.rearrange(
            "(h r q) (g u j) -> h u r q g j", h=2, r=64, q=NQ, g=NG, u=2, j=256
        )
        w_rows = original_weight.rearrange("(p q) k -> q p k", q=NQ)
        loads = load_list()
        slots = {"v1": 2, "v2": 2, "v3": 5, "p": 2, "x": 1}
        tiles = {}
        progress = {"loaded": 0, "transposed": 0, "held": 0, "combined": 0}

        def kind(n):
            return loads[n][0] + ("%d" % loads[n][3] if loads[n][0] == "v" else "")

        def start_loads():
            while progress["loaded"] < len(loads):
                n = progress["loaded"]
                same = [m for m in range(n) if kind(m) == kind(n)]
                if len(same) >= slots[kind(n)] and progress["transposed"] <= same[len(same) - slots[kind(n)]]:
                    return
                if loads[n][0] == "v":
                    h, q0, count = loads[n][1], loads[n][2], loads[n][3]
                    wt = wpool.tile([P, count * 1024], BF16, name="wt%d" % n, tag=kind(n), bufs=slots[kind(n)])
                    for u in range(2):
                        nc.sync.dma_start(
                            out=wt[u:P:2, :].rearrange("r (q g j) -> r q g j", q=count, g=NG, j=256),
                            in_=w_pairs[h, u, :, q0:q0 + count],
                        )
                elif loads[n][0] == "p":
                    wt = wpool.tile([P, 2048], BF16, name="wt%d" % n, tag="p", bufs=slots["p"])
                    nc.sync.dma_start(out=wt[:], in_=w_rows[loads[n][1]])
                else:
                    wt = wpool.tile([P, 2, 2048], BF16, name="x_sb")
                    nc.sync.dma_start(out=wt[:], in_=x.rearrange("(t m) k -> m t k", t=2))
                tiles[n] = wt
                progress["loaded"] = n + 1

        start_loads()

        s32 = const.tile([P, 1], F32, name="s32")
        nc.vector.tensor_copy(out=s32[:], in_=s_bc[:])
        gain = const.tile([P, NQ], F32, name="gain")
        nc.vector.tensor_scalar(
            out=gain[:], in0=b_bc[:], scalar1=s32[:, 0:1], scalar2=2.0, op0=ALU.mult, op1=ALU.mult
        )

        def transpose_planes(bank, words, b):
            for g2 in range(2):
                for u in range(2):
                    w0 = 256 * (2 * b + g2) + 128 * u
                    c0 = (g2 * 2 + u) * P
                    nc.tensor.transpose(out=bank[:, c0:c0 + P], in_=words[:, w0:w0 + P], identity=ident[:])

        def pair_up(bank, h):
            return bank[:].rearrange("p (g u h r) -> p h g r u", g=2, u=2, h=2, r=64)[:, h]

        def paired(words, b):
            return words[:, 2 * b * P:2 * (b + 1) * P].rearrange("p (g r u) -> p g r u", g=2, r=64, u=2)

        at = [const.tile([P, 1024], BF16, name="at%d" % h) for h in range(2)]
        pas = []
        for b in range(2):
            pa = axp.tile([P, 512], F32, name="pa%d" % b, tag="ax")
            transpose_planes(pa, a_sb[:].bitcast(F32), b)
            pas.append(pa)
        for h in range(2):
            nc.scalar.copy(out=paired(at[h][:].bitcast(F32), 0), in_=pair_up(pas[0], h))
            nc.vector.tensor_copy(out=paired(at[h][:].bitcast(F32), 1), in_=pair_up(pas[1], h))

        n_chunks = 2 * NQ // CHUNK
        grouped = []
        codes = []
        scales = []
        for c in range(n_chunks):
            grouped.append(gpool.tile([P, NG, CHUNK, 256], BF16, name="grouped%d" % c, align_bytes=64))
            codes.append(gpool.tile([P, NG, CHUNK * 64], U32, name="codes%d" % c, align_bytes=64))
            scales.append(gpool.tile([P, NG, CHUNK * 64], U8, name="scales%d" % c, align_bytes=64))

        def grouped_slice(h, q):
            return grouped[(h * NQ + q) // CHUNK][:, :, q % CHUNK, :]

        xg = const.tile([P, 4096], BF16, name="xg", align_bytes=64)
        x_codes = const.tile([P, 1024], U32, name="x_codes", align_bytes=64)
        x_scales = const.tile([P, 1024], U8, name="x_scales", align_bytes=64)

        def transpose_x(x_sb):
            for g in range(NG):
                px = axp.tile([P, 512], F32, name="px%d" % g, tag="ax")
                for u in range(2):
                    for t in range(2):
                        w0 = 256 * g + 128 * u
                        c0 = (u * 2 + t) * P
                        nc.tensor.transpose(
                            out=px[:, c0:c0 + P], in_=x_sb[:, t, :].bitcast(F32)[:, w0:w0 + P], identity=ident[:]
                        )
                nc.scalar.copy(
                    out=xg[:].bitcast(F32)[:, g * 512:(g + 1) * 512].rearrange("p (c u) -> p c u", u=2),
                    in_=px[:].rearrange("p (u c) -> p c u", u=2),
                )

        def combine_on_pool(q, wt):
            pq = []
            for b in range(2):
                bank = tpp.tile([P, 512], F32, name="pq%d_%d" % (q, b), tag="tp")
                transpose_planes(bank, wt[:].bitcast(F32), b)
                pq.append(bank)
            for h in range(2):
                delta = spool.tile([P, 1024], F32, name="delta%d_%d" % (q, h), tag="delta", bufs=3)
                nc.scalar.activation(out=delta[:], in_=at[h][:], func=ACT.Copy, scale=gain[:, q:q + 1])
                wts = spool.tile([P, 512], F32, name="wts%d_%d" % (q, h), tag="wts", bufs=4)
                for b in range(2):
                    nc.scalar.copy(out=paired(wts[:], b), in_=pair_up(pq[b], h))
                nc.gpsimd.tensor_tensor(
                    out=grouped_slice(h, q),
                    in0=wts[:].bitcast(BF16).rearrange("p (g j) -> p g j", g=NG),
                    in1=delta[:].rearrange("p (g j) -> p g j", g=NG),
                    op=ALU.add,
                )

        waiting = []

        def transpose_ahead():
            while progress["transposed"] < len(loads):
                n = progress["transposed"]
                need = {"v": loads[n][-1], "p": 2, "x": 0}[loads[n][0]]
                if progress["held"] + need > TP_BANKS:
                    return
                if loads[n][0] == "v":
                    h, q0, count = loads[n][1], loads[n][2], loads[n][3]
                    for k in range(count):
                        bank = tpp.tile([P, 512], F32, name="tp%d_%d" % (h, q0 + k), tag="tp")
                        for g in range(NG):
                            w0 = (k * NG + g) * P
                            nc.tensor.transpose(
                                out=bank[:, g * P:(g + 1) * P],
                                in_=tiles[n][:].bitcast(F32)[:, w0:w0 + P],
                                identity=ident[:],
                            )
                        waiting.append((h, q0 + k, bank))
                    progress["held"] += count
                elif loads[n][0] == "p":
                    combine_on_pool(loads[n][1], tiles[n])
                else:
                    transpose_x(tiles[n])
                progress["transposed"] = n + 1
                start_loads()

        transpose_ahead()
        while progress["combined"] < len(waiting):
            h, q, bank = waiting[progress["combined"]]
            progress["combined"] += 1
            nc.vector.scalar_tensor_tensor(
                out=grouped_slice(h, q),
                in0=at[h][:].rearrange("p (g j) -> p g j", g=NG),
                scalar=gain[:, q:q + 1],
                in1=bank[:].bitcast(BF16).rearrange("p (g j) -> p g j", g=NG),
                op0=ALU.mult,
                op1=ALU.add,
            )
            progress["held"] -= 1
            transpose_ahead()

        out_sb = {}
        for c in range(n_chunks):
            h, q0 = (c * CHUNK) // NQ, (c * CHUNK) % NQ
            accs = []
            for t in range(2):
                acc = tpp.tile([P, CHUNK * 64], F32, name="acc%d_%d" % (c, t), tag="tp")
                accs.append(acc)
            for g in range(NG):
                if c == 0:
                    nc.vector.quantize_mx(
                        out=x_codes[:, g * 256:(g + 1) * 256].bitcast(FP8X4),
                        scales=x_scales[:, g * 256:(g + 1) * 256],
                        in_=xg[:, g * 1024:(g + 1) * 1024],
                    )
                nc.vector.quantize_mx(
                    out=codes[c][:, g, :].bitcast(FP8X4),
                    scales=scales[c][:, g, :],
                    in_=grouped[c][:, g, :, :].rearrange("p q j -> p (q j)"),
                )
                for t in range(2):
                    m0 = g * 256 + t * P
                    nc.tensor.matmul_mx(
                        out=accs[t][:],
                        lhsT=x_codes[:, m0:m0 + P].bitcast(FP8X4),
                        lhsT_scale=x_scales[:, m0:m0 + P],
                        rhs=codes[c][:, g, :].bitcast(FP8X4),
                        rhs_scale=scales[c][:, g, :],
                        start=(g == 0),
                        stop=(g == NG - 1),
                    )
            for t in range(2):
                if q0 == 0:
                    out_sb[(h, t)] = opool.tile([P, 64, NQ], F32, name="out_sb%d%d" % (h, t))
                dst = out_sb[(h, t)][:, :, q0:q0 + CHUNK]
                src = accs[t][:].rearrange("m (q r) -> m r q", q=CHUNK)
                if c == n_chunks - 1 and t == 1:
                    nc.vector.tensor_copy(out=dst, in_=src)
                else:
                    nc.scalar.copy(out=dst, in_=src)
                if q0 + CHUNK == NQ:
                    nc.sync.dma_start(
                        out=out[t * P:(t + 1) * P, h * 1024:(h + 1) * 1024],
                        in_=out_sb[(h, t)][:].rearrange("m r q -> m (r q)"),
                    )
